import numpy as np
import ml_dtypes


def mxq(x, axis, fmt="e4m3"):
    dtype, down = {"e4m3": (ml_dtypes.float8_e4m3fn, 7), "e5m2": (ml_dtypes.float8_e5m2, 14)}[fmt]
    v = np.moveaxis(np.asarray(x, np.float32).astype(ml_dtypes.bfloat16).astype(np.float64), axis, -1)
    blocks = v.reshape(v.shape[:-1] + (-1, 32))
    amax = np.abs(blocks).max(-1, keepdims=True)
    byte = np.maximum(np.where(amax > 0, np.frexp(amax)[1] - 1 + 127, 0) - down, 1)
    scale = np.exp2(byte - 127.0)
    codes = (blocks / scale).astype(np.float32).astype(dtype).astype(np.float64)
    return np.moveaxis((codes * scale).reshape(v.shape), -1, axis)


WIDE = False


def mx_kscale(k):
    if not WIDE:
        return np.ones(k)
    levels = np.array([10, -10, 5, -5, 0])
    if k % 512:
        return np.exp2(np.random.permutation(np.resize(levels, k // 32))).repeat(32)
    a = np.empty((k // 512, 16))
    for p in range(k // 512):
        a[p, :8] = np.random.permutation(np.resize(levels, 8))
        for g in range(8):
            far = levels[np.abs(levels - a[p, g]) >= 10]
            a[p, g + 8] = far[np.random.randint(len(far))]
    return np.exp2(a.ravel()).repeat(32)


BF16 = ml_dtypes.bfloat16


def bf(x):
    return np.asarray(x, np.float32).astype(BF16)


def f64(x):
    return np.asarray(x).astype(np.float64)


B, T, D, F = 4, 32, 512, 256
K2, K3, K4 = 2, 3, 4
EPS = 1e-12


def conv_branch(xq, w, b):
    kw = w.shape[1]
    n = xq.shape[1] - kw + 1
    wq = mxq(f64(w), 2, "e4m3")
    out = sum((xq[:, k:k + n, :] @ wq[:, k, :].T) for k in range(kw))
    return np.maximum(out + f64(b), 0.0)


def l2norm(x, axis):
    n = np.sqrt(np.sum(x * x, axis=axis, keepdims=True))
    return x / np.maximum(n, EPS)


def setup_inputs():
    s = mx_kscale(D)
    return {"words_emb": bf(np.random.standard_normal((B, T, D)) * s),
            "W2": bf(np.random.standard_normal((F, K2, D)) / np.sqrt(K2 * D) / s), "b2": bf(np.random.standard_normal(F) * 0.3),
            "W3": bf(np.random.standard_normal((F, K3, D)) / np.sqrt(K3 * D) / s), "b3": bf(np.random.standard_normal(F) * 0.3),
            "W4": bf(np.random.standard_normal((F, K4, D)) / np.sqrt(K4 * D) / s), "b4": bf(np.random.standard_normal(F) * 0.3)}


def reference(words_emb, W2, b2, W3, b3, W4, b4):
    xq = mxq(f64(words_emb), 2, "e4m3")
    a = conv_branch(xq, W2, b2)
    b_ = conv_branch(xq, W3, b3)
    c = conv_branch(xq, W4, b4)
    seq = T - K4 + 1
    main = np.maximum(np.maximum(a[:, :seq], b_[:, :seq]), c[:, :seq])
    pen = np.maximum(a[:, seq], b_[:, seq])[:, None]
    last = a[:, seq + 1][:, None]
    code = np.concatenate([main, pen, last], axis=1)
    code = l2norm(code, 2)
    return code.transpose(0, 2, 1)

@@ -1,0 +1,212 @@
+from contextlib import ExitStack
+
+import concourse.mybir as mybir
+from concourse.masks import make_identity
+
+F32 = mybir.dt.float32
+BF16 = mybir.dt.bfloat16
+U32 = mybir.dt.uint32
+U8 = mybir.dt.uint8
+FP8X4 = mybir.dt.float8_e4m3fn_x4
+ALU = mybir.AluOpType
+ACT = mybir.ActivationFunctionType
+
+P = 128
+PACK = 4
+TEXTS, WORDS, FEATURES, FILTERS = 4, 32, 512, 256
+TOKENS = TEXTS * WORDS
+WIDTHS = (4, 3, 2)
+SHIFTS = max(WIDTHS)
+PARITIES = FILTERS // P
+POSITIONS = WORDS - min(WIDTHS) + 1
+EPS = 1e-12
+PAIRS = FEATURES // 2
+HALVES = PAIRS // P
+SLABS_PER_BANK = 2
+SLAB_COLS = P * PACK
+VECTOR_EMPTIES_EVERY = 4
+WARM_PASSES = 4
+WARM_COLS = 512
+CONV_LAG = 2
+
+assert TOKENS == P and FEATURES == P * PACK
+
+FLOPS = 2 * FEATURES * FILTERS * TEXTS * sum(w * (WORDS - w + 1) for w in WIDTHS)
+
+
+def tile_textheading_pa_s_kernel(tc, words_emb, W2, b2, W3, b3, W4, b4, out):
+    nc = tc.nc
+    weights = {2: W2, 3: W3, 4: W4}
+    biases = {2: b2, 3: b3, 4: b4}
+
+    first_slab = {}
+    n_slabs = 0
+    for width in WIDTHS:
+        first_slab[width] = n_slabs
+        n_slabs += PARITIES * width
+
+    with ExitStack() as ctx:
+        keep = ctx.enter_context(tc.tile_pool(name="keep", bufs=1))
+        flip = ctx.enter_context(tc.psum_pool(name="flip", bufs=4))
+        sums = ctx.enter_context(tc.psum_pool(name="sums", bufs=1))
+        ctx.enter_context(tc.manual_schedule())
+
+        b_rows = keep.tile([P, FILTERS], BF16)
+        nc.vector.memset(b_rows[:], 0.0)
+        for i, width in enumerate(WIDTHS):
+            nc.scalar.dma_start(out=b_rows[i : i + 1, :], in_=biases[width].rearrange("(o f) -> o f", o=1))
+        x_rows = keep.tile([P, FEATURES], BF16)
+        nc.sync.dma_start(out=x_rows[:], in_=words_emb.rearrange("n t d -> (n t) d"))
+        w_rows = []
+        for width in WIDTHS:
+            runs = weights[width].rearrange("(q j) k d -> q (j k d)", j=PARITIES)
+            for first in range(0, PARITIES * width * FEATURES, SLABS_PER_BANK * FEATURES):
+                rows = keep.tile([P, SLABS_PER_BANK * FEATURES], BF16, name="w_rows%d" % len(w_rows))
+                nc.sync.dma_start(out=rows[:], in_=runs[:, first : first + SLABS_PER_BANK * FEATURES])
+                w_rows.append(rows)
+
+        identity = keep.tile([P, P], F32)
+        make_identity(nc, identity[:])
+        ones = keep.tile([P, P], F32)
+        nc.vector.memset(ones[:], 1.0)
+        table_warmer = keep.tile([P, 1], F32)
+        nc.scalar.activation(out=table_warmer[:], in_=ones[:, 0:1], func=ACT.Abs_reciprocal_sqrt)
+
+        zeros = keep.tile([P, WARM_COLS * PACK], BF16, align_bytes=64)
+        zero_codes = keep.tile([P, WARM_COLS], U32, align_bytes=64)
+        zero_scales = keep.tile([P, WARM_COLS], U8, align_bytes=64)
+        nc.vector.memset(zeros[:].bitcast(F32), 0.0)
+        nc.vector.quantize_mx(out=zero_codes[:].bitcast(FP8X4), scales=zero_scales[:], in_=zeros[:])
+        idle_sums = flip.tile([P, WARM_COLS], F32, name="idle_sums", tag="flipped")
+        for i in range(WARM_PASSES):
+            nc.tensor.matmul_mx(
+                out=idle_sums[:],
+                lhsT=zero_codes[:, :P].bitcast(FP8X4),
+                lhsT_scale=zero_scales[:, :P],
+                rhs=zero_codes[:].bitcast(FP8X4),
+                rhs_scale=zero_scales[:],
+                start=True,
+                stop=True,
+            )
+
+        x_grouped = keep.tile([P, SHIFTS * TOKENS * PACK], BF16, align_bytes=64)
+        x_codes = keep.tile([P, SHIFTS * TOKENS], U32, align_bytes=64)
+        x_scales = keep.tile([P, SHIFTS * TOKENS], U8, align_bytes=64)
+        x_pairs = x_grouped[:].bitcast(F32).rearrange("p (s t u) -> p s t u", s=SHIFTS, u=HALVES)
+        nc.vector.memset(x_pairs[:, 1:, TOKENS - SHIFTS + 1 :, :], 0.0)
+        x_flipped = flip.tile([P, SLABS_PER_BANK * HALVES, P], F32, name="x_flipped", tag="flipped")
+        for u in range(HALVES):
+            nc.tensor.transpose(x_flipped[:, u, :], x_rows[:].bitcast(F32)[:, u::HALVES], identity[:])
+        nc.vector.tensor_copy(out=x_pairs[:, 0, :, :], in_=x_flipped[:, 0:HALVES, :].rearrange("p u t -> p t u"))
+        for s in range(1, SHIFTS):
+            nc.vector.tensor_copy(out=x_pairs[:, s, : TOKENS - s, :], in_=x_pairs[:, 0, s:, :])
+        nc.vector.quantize_mx(out=x_codes[:].bitcast(FP8X4), scales=x_scales[:], in_=x_grouped[:])
+
+        b_flipped = flip.tile([P, SLABS_PER_BANK * HALVES, P], F32, name="b_flipped", tag="flipped")
+        nc.tensor.transpose(b_flipped[:, 0, :], b_rows[:].bitcast(F32), identity[:])
+        bias = keep.tile([P, len(WIDTHS) * PARITIES], F32)
+        nc.vector.tensor_copy(out=bias[:], in_=b_flipped[:, 0, 0 : len(WIDTHS)].bitcast(BF16))
+
+        n_banks = n_slabs // SLABS_PER_BANK
+        w_grouped = []
+        w_codes = []
+        w_scales = []
+        for bank in range(n_banks):
+            w_grouped.append(keep.tile([P, SLABS_PER_BANK * SLAB_COLS], BF16, name="w_grouped%d" % bank, align_bytes=64))
+            w_codes.append(keep.tile([P, SLABS_PER_BANK * P], U32, name="w_codes%d" % bank, align_bytes=64))
+            w_scales.append(keep.tile([P, SLABS_PER_BANK * P], U8, name="w_scales%d" % bank, align_bytes=64))
+
+        def transpose(bank):
+            flipped = flip.tile([P, SLABS_PER_BANK * HALVES, P], F32, name="flipped", tag="flipped")
+            words = w_rows[bank][:].bitcast(F32)
+            for b in range(SLABS_PER_BANK):
+                for u in range(HALVES):
+                    every_other = words[:, b * PAIRS + u : (b + 1) * PAIRS : HALVES]
+                    nc.tensor.transpose(flipped[:, b * HALVES + u, :], every_other, identity[:])
+            pairs = w_grouped[bank][:].bitcast(F32).rearrange("p (b q u) -> p b q u", b=SLABS_PER_BANK, u=HALVES)
+            source = flipped[:].rearrange("p (b u) q -> p b q u", u=HALVES)
+            if bank % VECTOR_EMPTIES_EVERY == VECTOR_EMPTIES_EVERY - 1:
+                nc.vector.tensor_copy(out=pairs, in_=source)
+            else:
+                nc.scalar.copy(out=pairs, in_=source)
+
+        def quantise(bank):
+            nc.vector.quantize_mx(out=w_codes[bank][:].bitcast(FP8X4), scales=w_scales[bank][:], in_=w_grouped[bank][:])
+
+        code = keep.tile([P, PARITIES, TOKENS], F32)
+        nc.vector.memset(code[:], 0.0)
+
+        def by_text(ap, positions):
+            return ap.rearrange("q (n p) -> q n p", p=WORDS)[:, :, :positions]
+
+        conv = {}
+        for width in WIDTHS:
+            conv[width] = sums.tile([P, PARITIES, TOKENS], F32, name="conv%d" % width)
+
+        def convolve(width):
+            for j in range(PARITIES):
+                for k in range(width):
+                    bank, place = divmod(first_slab[width] + j * width + k, SLABS_PER_BANK)
+                    slab = slice(place * P, (place + 1) * P)
+                    shifted = slice(k * TOKENS, (k + 1) * TOKENS)
+                    nc.tensor.matmul_mx(
+                        out=conv[width][:, j, :],
+                        lhsT=w_codes[bank][:, slab].bitcast(FP8X4),
+                        lhsT_scale=w_scales[bank][:, slab],
+                        rhs=x_codes[:, shifted].bitcast(FP8X4),
+                        rhs_scale=x_scales[:, shifted],
+                        start=(k == 0),
+                        stop=(k == width - 1),
+                    )
+
+        def merge(width):
+            positions = WORDS - width + 1
+            for j in range(PARITIES):
+                column = WIDTHS.index(width) * PARITIES + j
+                nc.vector.scalar_tensor_tensor(
+                    out=by_text(code[:, j, :], positions),
+                    in0=by_text(conv[width][:, j, :], positions),
+                    scalar=bias[:, column : column + 1],
+                    in1=by_text(code[:, j, :], positions),
+                    op0=ALU.add,
+                    op1=ALU.max,
+                )
+
+        last_bank = {}
+        for width in WIDTHS:
+            last_bank[(first_slab[width] + PARITIES * width) // SLABS_PER_BANK - 1] = width
+        for step in range(n_banks + CONV_LAG + 1):
+            if step < n_banks:
+                transpose(step)
+            if 0 <= step - 1 < n_banks:
+                quantise(step - 1)
+            if step - CONV_LAG in last_bank:
+                convolve(last_bank[step - CONV_LAG])
+            if step - CONV_LAG - 1 in last_bank:
+                merge(last_bank[step - CONV_LAG - 1])
+
+        squares = keep.tile([P, PARITIES, TOKENS], F32)
+        square_sum = sums.tile([P, TOKENS], F32)
+        for j in range(PARITIES):
+            nc.scalar.activation(out=squares[:, j, :], in_=code[:, j, :], func=ACT.Square)
+            nc.tensor.matmul(
+                out=square_sum[:], lhsT=ones[:], rhs=squares[:, j, :], start=(j == 0), stop=(j == PARITIES - 1)
+            )
+        inverse_norm = keep.tile([P, TOKENS], F32)
+        nc.scalar.activation(
+            out=by_text(inverse_norm[:], POSITIONS), in_=by_text(square_sum[:], POSITIONS), func=ACT.Abs_reciprocal_sqrt
+        )
+        result = keep.tile([P, TEXTS, PARITIES, POSITIONS], F32)
+        for j in range(PARITIES):
+            nc.vector.scalar_tensor_tensor(
+                out=result[:, :, j, :],
+                in0=by_text(inverse_norm[:], POSITIONS),
+                scalar=1.0 / EPS,
+                in1=by_text(code[:, j, :], POSITIONS),
+                op0=ALU.min,
+                op1=ALU.mult,
+            )
+        nc.sync.dma_start(
+            out=out.rearrange("n (q j) p -> q n (j p)", j=PARITIES),
+            in_=result[:].rearrange("q n j p -> q n (j p)"),
+        )

@@ -27,6 +27,8 @@ SLAB_COLS = P * PACK
 VECTOR_EMPTIES_EVERY = 4
 WARM_PASSES = 4
 WARM_COLS = 512
+BLOCK = 32
+SPREAD = P // BLOCK
 CONV_LAG = 2
 
 assert TOKENS == P and FEATURES == P * PACK
@@ -67,10 +69,15 @@ def tile_textheading_pa_s_kernel(tc, words_emb, W2, b2, W3, b3, W4, b4, out):
 
         identity = keep.tile([P, P], F32)
         make_identity(nc, identity[:])
-        ones = keep.tile([P, P], F32)
+        ones = keep.tile([P, 1], F32)
         nc.vector.memset(ones[:], 1.0)
+        permutation = keep.tile([P, P], F32)
+        nc.gpsimd.tensor_copy(
+            out=permutation[:].rearrange("p (c i) -> p c i", c=SPREAD),
+            in_=identity[:].rearrange("p (i c) -> p c i", c=SPREAD),
+        )
         table_warmer = keep.tile([P, 1], F32)
-        nc.scalar.activation(out=table_warmer[:], in_=ones[:, 0:1], func=ACT.Abs_reciprocal_sqrt)
+        nc.scalar.activation(out=table_warmer[:], in_=ones[:], func=ACT.Abs_reciprocal_sqrt)
 
         zeros = keep.tile([P, WARM_COLS * PACK], BF16, align_bytes=64)
         zero_codes = keep.tile([P, WARM_COLS], U32, align_bytes=64)
@@ -135,6 +142,7 @@ def tile_textheading_pa_s_kernel(tc, words_emb, W2, b2, W3, b3, W4, b4, out):
 
         code = keep.tile([P, PARITIES, TOKENS], F32)
         nc.vector.memset(code[:], 0.0)
+        nc.vector.memset(code[:].rearrange("q j (n p) -> q j n p", p=WORDS)[:, :, :, POSITIONS:], 1.0)
 
         def by_text(ap, positions):
             return ap.rearrange("q (n p) -> q n p", p=WORDS)[:, :, :positions]
@@ -185,28 +193,34 @@ def tile_textheading_pa_s_kernel(tc, words_emb, W2, b2, W3, b3, W4, b4, out):
             if step - CONV_LAG - 1 in last_bank:
                 merge(last_bank[step - CONV_LAG - 1])
 
-        squares = keep.tile([P, PARITIES, TOKENS], F32)
-        square_sum = sums.tile([P, TOKENS], F32)
+        turned = sums.tile([P, PARITIES, P], F32)
+        blocks = keep.tile([P, PARITIES, P], F32, align_bytes=64)
         for j in range(PARITIES):
-            nc.scalar.activation(out=squares[:, j, :], in_=code[:, j, :], func=ACT.Square)
-            nc.tensor.matmul(
-                out=square_sum[:], lhsT=ones[:], rhs=squares[:, j, :], start=(j == 0), stop=(j == PARITIES - 1)
-            )
-        inverse_norm = keep.tile([P, TOKENS], F32)
+            nc.tensor.transpose(turned[:, j, :], code[:, j, :], permutation[:])
+        for j in range(PARITIES):
+            nc.vector.transpose(blocks[:, j, :], turned[:, j, :])
+        squares = keep.tile([P, PARITIES * P], F32)
+        square_sum = keep.tile([P, 1], F32)
         nc.scalar.activation(
-            out=by_text(inverse_norm[:], POSITIONS), in_=by_text(square_sum[:], POSITIONS), func=ACT.Abs_reciprocal_sqrt
+            out=squares[:], in_=turned[:].rearrange("t j f -> t (j f)"), func=ACT.Square, accum_out=square_sum[:]
         )
-        result = keep.tile([P, TEXTS, PARITIES, POSITIONS], F32)
+        inverse_norm = keep.tile([P, BLOCK], F32, align_bytes=64)
+        nc.scalar.activation(
+            out=inverse_norm[:], in_=square_sum[:].to_broadcast([P, BLOCK]), func=ACT.Abs_reciprocal_sqrt
+        )
+        inverse_by_position = keep.tile([P, BLOCK], F32, align_bytes=64)
+        nc.vector.transpose(inverse_by_position[:], inverse_norm[:])
+        result = keep.tile([P, SPREAD, PARITIES, POSITIONS], F32)
         for j in range(PARITIES):
             nc.vector.scalar_tensor_tensor(
                 out=result[:, :, j, :],
-                in0=by_text(inverse_norm[:], POSITIONS),
+                in0=inverse_by_position[:, :POSITIONS].unsqueeze(1).to_broadcast([P, SPREAD, POSITIONS]),
                 scalar=1.0 / EPS,
-                in1=by_text(code[:, j, :], POSITIONS),
+                in1=blocks[:, j, :].rearrange("q (c p) -> q c p", p=BLOCK)[:, :, :POSITIONS],
                 op0=ALU.min,
                 op1=ALU.mult,
             )
         nc.sync.dma_start(
-            out=out.rearrange("n (q j) p -> q n (j p)", j=PARITIES),
-            in_=result[:].rearrange("q n j p -> q n (j p)"),
+            out=out.rearrange("n (i b) p -> (n i) (b p)", i=BLOCK),
+            in_=result[:].rearrange("q c j p -> q (c j p)"),
         )

@@ -24,9 +24,9 @@ PAIRS = FEATURES // 2
 HALVES = PAIRS // P
 SLABS_PER_BANK = 2
 SLAB_COLS = P * PACK
-VECTOR_EMPTIES_EVERY = 4
-WARM_PASSES = 4
-WARM_COLS = 512
+VECTOR_EMPTIES = (7,)
+WARM_PASSES = 12
+BANKS_BEFORE_BIASES = 5
 BLOCK = 32
 SPREAD = P // BLOCK
 CONV_LAG = 2
@@ -49,16 +49,19 @@ def tile_textheading_pa_s_kernel(tc, words_emb, W2, b2, W3, b3, W4, b4, out):
 
     with ExitStack() as ctx:
         keep = ctx.enter_context(tc.tile_pool(name="keep", bufs=1))
-        flip = ctx.enter_context(tc.psum_pool(name="flip", bufs=4))
+        flip = ctx.enter_context(tc.psum_pool(name="flip", bufs=5))
         sums = ctx.enter_context(tc.psum_pool(name="sums", bufs=1))
         ctx.enter_context(tc.manual_schedule())
 
-        b_rows = keep.tile([P, FILTERS], BF16)
-        nc.vector.memset(b_rows[:], 0.0)
-        for i, width in enumerate(WIDTHS):
-            nc.scalar.dma_start(out=b_rows[i : i + 1, :], in_=biases[width].rearrange("(o f) -> o f", o=1))
         x_rows = keep.tile([P, FEATURES], BF16)
         nc.sync.dma_start(out=x_rows[:], in_=words_emb.rearrange("n t d -> (n t) d"))
+        b_rows = keep.tile([P, FILTERS], BF16)
+        nc.vector.memset(b_rows[:].bitcast(F32), 0.0)
+
+        def load_biases():
+            for i, width in enumerate(WIDTHS):
+                nc.sync.dma_start(out=b_rows[i : i + 1, :], in_=biases[width].rearrange("(o f) -> o f", o=1))
+
         w_rows = []
         for width in WIDTHS:
             runs = weights[width].rearrange("(q j) k d -> q (j k d)", j=PARITIES)
@@ -66,6 +69,25 @@ def tile_textheading_pa_s_kernel(tc, words_emb, W2, b2, W3, b3, W4, b4, out):
                 rows = keep.tile([P, SLABS_PER_BANK * FEATURES], BF16, name="w_rows%d" % len(w_rows))
                 nc.sync.dma_start(out=rows[:], in_=runs[:, first : first + SLABS_PER_BANK * FEATURES])
                 w_rows.append(rows)
+                if len(w_rows) == BANKS_BEFORE_BIASES:
+                    load_biases()
+
+        zeros = keep.tile([P, P * PACK], BF16, align_bytes=64)
+        zero_codes = keep.tile([P, P], U32, align_bytes=64)
+        zero_scales = keep.tile([P, P], U8, align_bytes=64)
+        nc.vector.memset(zeros[:].bitcast(F32), 0.0)
+        nc.vector.quantize_mx(out=zero_codes[:].bitcast(FP8X4), scales=zero_scales[:], in_=zeros[:])
+        idle_sums = flip.tile([P, P], F32, name="idle_sums", tag="flipped")
+        for i in range(WARM_PASSES):
+            nc.tensor.matmul_mx(
+                out=idle_sums[:],
+                lhsT=zero_codes[:].bitcast(FP8X4),
+                lhsT_scale=zero_scales[:],
+                rhs=zero_codes[:].bitcast(FP8X4),
+                rhs_scale=zero_scales[:],
+                start=True,
+                stop=True,
+            )
 
         identity = keep.tile([P, P], F32)
         make_identity(nc, identity[:])
@@ -79,40 +101,21 @@ def tile_textheading_pa_s_kernel(tc, words_emb, W2, b2, W3, b3, W4, b4, out):
         table_warmer = keep.tile([P, 1], F32)
         nc.scalar.activation(out=table_warmer[:], in_=ones[:], func=ACT.Abs_reciprocal_sqrt)
 
-        zeros = keep.tile([P, WARM_COLS * PACK], BF16, align_bytes=64)
-        zero_codes = keep.tile([P, WARM_COLS], U32, align_bytes=64)
-        zero_scales = keep.tile([P, WARM_COLS], U8, align_bytes=64)
-        nc.vector.memset(zeros[:].bitcast(F32), 0.0)
-        nc.vector.quantize_mx(out=zero_codes[:].bitcast(FP8X4), scales=zero_scales[:], in_=zeros[:])
-        idle_sums = flip.tile([P, WARM_COLS], F32, name="idle_sums", tag="flipped")
-        for i in range(WARM_PASSES):
-            nc.tensor.matmul_mx(
-                out=idle_sums[:],
-                lhsT=zero_codes[:, :P].bitcast(FP8X4),
-                lhsT_scale=zero_scales[:, :P],
-                rhs=zero_codes[:].bitcast(FP8X4),
-                rhs_scale=zero_scales[:],
-                start=True,
-                stop=True,
-            )
-
         x_grouped = keep.tile([P, SHIFTS * TOKENS * PACK], BF16, align_bytes=64)
         x_codes = keep.tile([P, SHIFTS * TOKENS], U32, align_bytes=64)
         x_scales = keep.tile([P, SHIFTS * TOKENS], U8, align_bytes=64)
         x_pairs = x_grouped[:].bitcast(F32).rearrange("p (s t u) -> p s t u", s=SHIFTS, u=HALVES)
         nc.vector.memset(x_pairs[:, 1:, TOKENS - SHIFTS + 1 :, :], 0.0)
-        x_flipped = flip.tile([P, SLABS_PER_BANK * HALVES, P], F32, name="x_flipped", tag="flipped")
-        for u in range(HALVES):
-            nc.tensor.transpose(x_flipped[:, u, :], x_rows[:].bitcast(F32)[:, u::HALVES], identity[:])
-        nc.vector.tensor_copy(out=x_pairs[:, 0, :, :], in_=x_flipped[:, 0:HALVES, :].rearrange("p u t -> p t u"))
-        for s in range(1, SHIFTS):
-            nc.vector.tensor_copy(out=x_pairs[:, s, : TOKENS - s, :], in_=x_pairs[:, 0, s:, :])
+        x_flipped = []
+        for copy in (nc.vector.tensor_copy, nc.scalar.copy):
+            flipped = flip.tile([P, SLABS_PER_BANK * HALVES, P], F32, name="x_flipped", tag="flipped")
+            for u in range(HALVES):
+                nc.tensor.transpose(flipped[:, u, :], x_rows[:].bitcast(F32)[:, u::HALVES], identity[:])
+            x_flipped.append((copy, flipped))
+        for s in range(SHIFTS):
+            copy, flipped = x_flipped[s % len(x_flipped)]
+            copy(out=x_pairs[:, s, : TOKENS - s, :], in_=flipped[:, 0:HALVES, s:].rearrange("p u t -> p t u"))
         nc.vector.quantize_mx(out=x_codes[:].bitcast(FP8X4), scales=x_scales[:], in_=x_grouped[:])
-
-        b_flipped = flip.tile([P, SLABS_PER_BANK * HALVES, P], F32, name="b_flipped", tag="flipped")
-        nc.tensor.transpose(b_flipped[:, 0, :], b_rows[:].bitcast(F32), identity[:])
-        bias = keep.tile([P, len(WIDTHS) * PARITIES], F32)
-        nc.vector.tensor_copy(out=bias[:], in_=b_flipped[:, 0, 0 : len(WIDTHS)].bitcast(BF16))
 
         n_banks = n_slabs // SLABS_PER_BANK
         w_grouped = []
@@ -125,24 +128,47 @@ def tile_textheading_pa_s_kernel(tc, words_emb, W2, b2, W3, b3, W4, b4, out):
 
         def transpose(bank):
             flipped = flip.tile([P, SLABS_PER_BANK * HALVES, P], F32, name="flipped", tag="flipped")
-            words = w_rows[bank][:].bitcast(F32)
             for b in range(SLABS_PER_BANK):
-                for u in range(HALVES):
-                    every_other = words[:, b * PAIRS + u : (b + 1) * PAIRS : HALVES]
-                    nc.tensor.transpose(flipped[:, b * HALVES + u, :], every_other, identity[:])
+                transpose_slab(bank, b, flipped[:, b * HALVES : (b + 1) * HALVES, :])
             pairs = w_grouped[bank][:].bitcast(F32).rearrange("p (b q u) -> p b q u", b=SLABS_PER_BANK, u=HALVES)
-            source = flipped[:].rearrange("p (b u) q -> p b q u", u=HALVES)
-            if bank % VECTOR_EMPTIES_EVERY == VECTOR_EMPTIES_EVERY - 1:
-                nc.vector.tensor_copy(out=pairs, in_=source)
-            else:
-                nc.scalar.copy(out=pairs, in_=source)
+            copy = nc.vector.tensor_copy if bank in VECTOR_EMPTIES else nc.scalar.copy
+            copy(out=pairs, in_=flipped[:].rearrange("p (b u) q -> p b q u", u=HALVES))
 
-        def quantise(bank):
-            nc.vector.quantize_mx(out=w_codes[bank][:].bitcast(FP8X4), scales=w_scales[bank][:], in_=w_grouped[bank][:])
+        def transpose_slab(bank, b, flipped):
+            words = w_rows[bank][:].bitcast(F32)
+            for u in range(HALVES):
+                nc.tensor.transpose(flipped[:, u, :], words[:, b * PAIRS + u : (b + 1) * PAIRS : HALVES], identity[:])
 
-        code = keep.tile([P, PARITIES, TOKENS], F32)
-        nc.vector.memset(code[:], 0.0)
-        nc.vector.memset(code[:].rearrange("q j (n p) -> q j n p", p=WORDS)[:, :, :, POSITIONS:], 1.0)
+        def transpose_in_halves(bank):
+            for b, copy in enumerate((nc.scalar.copy, nc.vector.tensor_copy)):
+                flipped = flip.tile([P, SLABS_PER_BANK * HALVES, P], F32, name="half", tag="flipped")
+                transpose_slab(bank, b, flipped[:, 0:HALVES, :])
+                pairs = w_grouped[bank][:, b * SLAB_COLS : (b + 1) * SLAB_COLS].bitcast(F32)
+                copy(
+                    out=pairs.rearrange("p (q u) -> p q u", u=HALVES),
+                    in_=flipped[:, 0:HALVES, :].rearrange("p u q -> p q u"),
+                )
+
+        def quantise(bank, slabs=(0, SLABS_PER_BANK)):
+            first, end = slabs
+            nc.vector.quantize_mx(
+                out=w_codes[bank][:, first * P : end * P].bitcast(FP8X4),
+                scales=w_scales[bank][:, first * P : end * P],
+                in_=w_grouped[bank][:, first * SLAB_COLS : end * SLAB_COLS],
+            )
+
+        bias = keep.tile([P, len(WIDTHS) * PARITIES], F32)
+
+        def turn_biases():
+            b_flipped = flip.tile([P, SLABS_PER_BANK * HALVES, P], F32, name="b_flipped", tag="flipped")
+            nc.tensor.transpose(b_flipped[:, 0, :], b_rows[:].bitcast(F32), identity[:])
+            nc.vector.tensor_copy(out=bias[:], in_=b_flipped[:, 0, 0 : len(WIDTHS)].bitcast(BF16))
+
+        code = []
+        for j in range(PARITIES):
+            code.append(keep.tile([P, TOKENS], F32, name="code%d" % j))
+            nc.vector.memset(code[j][:], 0.0)
+            nc.vector.memset(code[j][:].rearrange("q (n p) -> q n p", p=WORDS)[:, :, POSITIONS:], 1.0)
 
         def by_text(ap, positions):
             return ap.rearrange("q (n p) -> q n p", p=WORDS)[:, :, :positions]
@@ -151,58 +177,77 @@ def tile_textheading_pa_s_kernel(tc, words_emb, W2, b2, W3, b3, W4, b4, out):
         for width in WIDTHS:
             conv[width] = sums.tile([P, PARITIES, TOKENS], F32, name="conv%d" % width)
 
-        def convolve(width):
-            for j in range(PARITIES):
-                for k in range(width):
-                    bank, place = divmod(first_slab[width] + j * width + k, SLABS_PER_BANK)
-                    slab = slice(place * P, (place + 1) * P)
-                    shifted = slice(k * TOKENS, (k + 1) * TOKENS)
-                    nc.tensor.matmul_mx(
-                        out=conv[width][:, j, :],
-                        lhsT=w_codes[bank][:, slab].bitcast(FP8X4),
-                        lhsT_scale=w_scales[bank][:, slab],
-                        rhs=x_codes[:, shifted].bitcast(FP8X4),
-                        rhs_scale=x_scales[:, shifted],
-                        start=(k == 0),
-                        stop=(k == width - 1),
-                    )
-
-        def merge(width):
-            positions = WORDS - width + 1
-            for j in range(PARITIES):
-                column = WIDTHS.index(width) * PARITIES + j
-                nc.vector.scalar_tensor_tensor(
-                    out=by_text(code[:, j, :], positions),
-                    in0=by_text(conv[width][:, j, :], positions),
-                    scalar=bias[:, column : column + 1],
-                    in1=by_text(code[:, j, :], positions),
-                    op0=ALU.add,
-                    op1=ALU.max,
+        def convolve(width, j):
+            for k in range(width):
+                bank, place = divmod(first_slab[width] + j * width + k, SLABS_PER_BANK)
+                slab = slice(place * P, (place + 1) * P)
+                shifted = slice(k * TOKENS, (k + 1) * TOKENS)
+                nc.tensor.matmul_mx(
+                    out=conv[width][:, j, :],
+                    lhsT=w_codes[bank][:, slab].bitcast(FP8X4),
+                    lhsT_scale=w_scales[bank][:, slab],
+                    rhs=x_codes[:, shifted].bitcast(FP8X4),
+                    rhs_scale=x_scales[:, shifted],
+                    start=(k == 0),
+                    stop=(k == width - 1),
                 )
 
+        def merge(width, j):
+            positions = WORDS - width + 1
+            column = WIDTHS.index(width) * PARITIES + j
+            nc.vector.scalar_tensor_tensor(
+                out=by_text(code[j][:], positions),
+                in0=by_text(conv[width][:, j, :], positions),
+                scalar=bias[:, column : column + 1],
+                in1=by_text(code[j][:], positions),
+                op0=ALU.add,
+                op1=ALU.max,
+            )
+
+        widest, middle, narrowest = WIDTHS
         last_bank = {}
         for width in WIDTHS:
-            last_bank[(first_slab[width] + PARITIES * width) // SLABS_PER_BANK - 1] = width
-        for step in range(n_banks + CONV_LAG + 1):
-            if step < n_banks:
+            last_bank[width] = (first_slab[width] + PARITIES * width) // SLABS_PER_BANK - 1
+        for step in range(n_banks):
+            if step < n_banks - 1:
                 transpose(step)
-            if 0 <= step - 1 < n_banks:
+            else:
+                transpose_in_halves(step)
+            if step == last_bank[widest]:
+                turn_biases()
+            if step >= 1:
                 quantise(step - 1)
-            if step - CONV_LAG in last_bank:
-                convolve(last_bank[step - CONV_LAG])
-            if step - CONV_LAG - 1 in last_bank:
-                merge(last_bank[step - CONV_LAG - 1])
+            for j in range(PARITIES):
+                if step == last_bank[widest] + CONV_LAG:
+                    convolve(widest, j)
+                if step == last_bank[widest] + CONV_LAG + 1:
+                    merge(widest, j)
+                if step == last_bank[middle] + CONV_LAG:
+                    convolve(middle, j)
+        convolve(narrowest, 0)
+        for b in range(SLABS_PER_BANK):
+            quantise(n_banks - 1, (b, b + 1))
+        convolve(narrowest, 1)
+        for j in range(PARITIES):
+            merge(middle, j)
+        for j in range(PARITIES):
+            merge(narrowest, j)
 
-        turned = sums.tile([P, PARITIES, P], F32)
+        turned_for_scalar = sums.tile([P, PARITIES, P], F32, name="turned_for_scalar", tag="conv%d" % WIDTHS[0])
+        turned_for_vector = sums.tile([P, PARITIES, P], F32, name="turned_for_vector", tag="conv%d" % WIDTHS[1])
         blocks = keep.tile([P, PARITIES, P], F32, align_bytes=64)
+        for turned in (turned_for_scalar, turned_for_vector):
+            for j in range(PARITIES):
+                nc.tensor.transpose(turned[:, j, :], code[j][:], permutation[:])
         for j in range(PARITIES):
-            nc.tensor.transpose(turned[:, j, :], code[:, j, :], permutation[:])
-        for j in range(PARITIES):
-            nc.vector.transpose(blocks[:, j, :], turned[:, j, :])
+            nc.vector.transpose(blocks[:, j, :], turned_for_vector[:, j, :])
         squares = keep.tile([P, PARITIES * P], F32)
         square_sum = keep.tile([P, 1], F32)
         nc.scalar.activation(
-            out=squares[:], in_=turned[:].rearrange("t j f -> t (j f)"), func=ACT.Square, accum_out=square_sum[:]
+            out=squares[:],
+            in_=turned_for_scalar[:].rearrange("t j f -> t (j f)"),
+            func=ACT.Square,
+            accum_out=square_sum[:],
         )
         inverse_norm = keep.tile([P, BLOCK], F32, align_bytes=64)
         nc.scalar.activation(

@@ -24,12 +24,11 @@ PAIRS = FEATURES // 2
 HALVES = PAIRS // P
 SLABS_PER_BANK = 2
 SLAB_COLS = P * PACK
-VECTOR_EMPTIES = (7,)
-WARM_PASSES = 12
+WARM_PASSES = 8
 BANKS_BEFORE_BIASES = 5
 BLOCK = 32
 SPREAD = P // BLOCK
-CONV_LAG = 2
+CONV_LAG = {4: 3, 3: 2}
 
 assert TOKENS == P and FEATURES == P * PACK
 
@@ -131,8 +130,7 @@ def tile_textheading_pa_s_kernel(tc, words_emb, W2, b2, W3, b3, W4, b4, out):
             for b in range(SLABS_PER_BANK):
                 transpose_slab(bank, b, flipped[:, b * HALVES : (b + 1) * HALVES, :])
             pairs = w_grouped[bank][:].bitcast(F32).rearrange("p (b q u) -> p b q u", b=SLABS_PER_BANK, u=HALVES)
-            copy = nc.vector.tensor_copy if bank in VECTOR_EMPTIES else nc.scalar.copy
-            copy(out=pairs, in_=flipped[:].rearrange("p (b u) q -> p b q u", u=HALVES))
+            nc.scalar.copy(out=pairs, in_=flipped[:].rearrange("p (b u) q -> p b q u", u=HALVES))
 
         def transpose_slab(bank, b, flipped):
             words = w_rows[bank][:].bitcast(F32)
@@ -218,11 +216,11 @@ def tile_textheading_pa_s_kernel(tc, words_emb, W2, b2, W3, b3, W4, b4, out):
             if step >= 1:
                 quantise(step - 1)
             for j in range(PARITIES):
-                if step == last_bank[widest] + CONV_LAG:
+                if step == last_bank[widest] + CONV_LAG[widest]:
                     convolve(widest, j)
-                if step == last_bank[widest] + CONV_LAG + 1:
+                if step == last_bank[widest] + CONV_LAG[widest] + 1:
                     merge(widest, j)
-                if step == last_bank[middle] + CONV_LAG:
+                if step == last_bank[middle] + CONV_LAG[middle]:
                     convolve(middle, j)
         convolve(narrowest, 0)
         for b in range(SLABS_PER_BANK):
@@ -230,28 +228,28 @@ def tile_textheading_pa_s_kernel(tc, words_emb, W2, b2, W3, b3, W4, b4, out):
         convolve(narrowest, 1)
         for j in range(PARITIES):
             merge(middle, j)
-        for j in range(PARITIES):
             merge(narrowest, j)
 
-        turned_for_scalar = sums.tile([P, PARITIES, P], F32, name="turned_for_scalar", tag="conv%d" % WIDTHS[0])
-        turned_for_vector = sums.tile([P, PARITIES, P], F32, name="turned_for_vector", tag="conv%d" % WIDTHS[1])
         blocks = keep.tile([P, PARITIES, P], F32, align_bytes=64)
-        for turned in (turned_for_scalar, turned_for_vector):
-            for j in range(PARITIES):
-                nc.tensor.transpose(turned[:, j, :], code[j][:], permutation[:])
+        squares = keep.tile([P, PARITIES, P], F32)
+        square_sum = []
         for j in range(PARITIES):
-            nc.vector.transpose(blocks[:, j, :], turned_for_vector[:, j, :])
-        squares = keep.tile([P, PARITIES * P], F32)
-        square_sum = keep.tile([P, 1], F32)
-        nc.scalar.activation(
-            out=squares[:],
-            in_=turned_for_scalar[:].rearrange("t j f -> t (j f)"),
-            func=ACT.Square,
-            accum_out=square_sum[:],
-        )
+            square_sum.append(keep.tile([P, 1], F32, name="square_sum%d" % j))
+        for j in range(PARITIES):
+            turned_for_scalar = flip.tile([P, P], F32, name="turned_for_scalar", tag="flipped")
+            turned_for_vector = flip.tile([P, P], F32, name="turned_for_vector", tag="flipped")
+            for turned in (turned_for_scalar, turned_for_vector):
+                nc.tensor.transpose(turned[:], code[j][:], permutation[:])
+            nc.vector.transpose(blocks[:, j, :], turned_for_vector[:])
+            nc.scalar.activation(
+                out=squares[:, j, :], in_=turned_for_scalar[:], func=ACT.Square, accum_out=square_sum[j][:]
+            )
         inverse_norm = keep.tile([P, BLOCK], F32, align_bytes=64)
         nc.scalar.activation(
-            out=inverse_norm[:], in_=square_sum[:].to_broadcast([P, BLOCK]), func=ACT.Abs_reciprocal_sqrt
+            out=inverse_norm[:],
+            in_=square_sum[1][:].to_broadcast([P, BLOCK]),
+            func=ACT.Abs_reciprocal_sqrt,
+            bias=square_sum[0][:],
         )
         inverse_by_position = keep.tile([P, BLOCK], F32, align_bytes=64)
         nc.vector.transpose(inverse_by_position[:], inverse_norm[:])

@@ -24,11 +24,12 @@ PAIRS = FEATURES // 2
 HALVES = PAIRS // P
 SLABS_PER_BANK = 2
 SLAB_COLS = P * PACK
-WARM_PASSES = 8
+WARM_PASSES = 12
 BANKS_BEFORE_BIASES = 5
 BLOCK = 32
 SPREAD = P // BLOCK
-CONV_LAG = {4: 3, 3: 2}
+CONV_LAG = 2
+MERGE_STEP = 6
 
 assert TOKENS == P and FEATURES == P * PACK
 
@@ -97,6 +98,12 @@ def tile_textheading_pa_s_kernel(tc, words_emb, W2, b2, W3, b3, W4, b4, out):
             out=permutation[:].rearrange("p (c i) -> p c i", c=SPREAD),
             in_=identity[:].rearrange("p (i c) -> p c i", c=SPREAD),
         )
+        code = []
+        for j in range(PARITIES):
+            code.append(keep.tile([P, TOKENS], F32, name="code%d" % j))
+            nc.vector.memset(code[j][:], 0.0)
+        for j in range(PARITIES):
+            nc.vector.memset(code[j][:].rearrange("q (n p) -> q n p", p=WORDS)[:, :, POSITIONS:], 1.0)
         table_warmer = keep.tile([P, 1], F32)
         nc.scalar.activation(out=table_warmer[:], in_=ones[:], func=ACT.Abs_reciprocal_sqrt)
 
@@ -162,12 +169,6 @@ def tile_textheading_pa_s_kernel(tc, words_emb, W2, b2, W3, b3, W4, b4, out):
             nc.tensor.transpose(b_flipped[:, 0, :], b_rows[:].bitcast(F32), identity[:])
             nc.vector.tensor_copy(out=bias[:], in_=b_flipped[:, 0, 0 : len(WIDTHS)].bitcast(BF16))
 
-        code = []
-        for j in range(PARITIES):
-            code.append(keep.tile([P, TOKENS], F32, name="code%d" % j))
-            nc.vector.memset(code[j][:], 0.0)
-            nc.vector.memset(code[j][:].rearrange("q (n p) -> q n p", p=WORDS)[:, :, POSITIONS:], 1.0)
-
         def by_text(ap, positions):
             return ap.rearrange("q (n p) -> q n p", p=WORDS)[:, :, :positions]
 
@@ -203,25 +204,27 @@ def tile_textheading_pa_s_kernel(tc, words_emb, W2, b2, W3, b3, W4, b4, out):
             )
 
         widest, middle, narrowest = WIDTHS
-        last_bank = {}
+        due = {}
         for width in WIDTHS:
-            last_bank[width] = (first_slab[width] + PARITIES * width) // SLABS_PER_BANK - 1
+            for j in range(PARITIES):
+                last_slab = first_slab[width] + (j + 1) * width - 1
+                due[width, j] = last_slab // SLABS_PER_BANK + CONV_LAG
         for step in range(n_banks):
             if step < n_banks - 1:
                 transpose(step)
             else:
                 transpose_in_halves(step)
-            if step == last_bank[widest]:
+            if step == MERGE_STEP - 1:
                 turn_biases()
             if step >= 1:
                 quantise(step - 1)
-            for j in range(PARITIES):
-                if step == last_bank[widest] + CONV_LAG[widest]:
-                    convolve(widest, j)
-                if step == last_bank[widest] + CONV_LAG[widest] + 1:
+            for width in (widest, middle):
+                for j in range(PARITIES):
+                    if step == due[width, j]:
+                        convolve(width, j)
+            if step == MERGE_STEP:
+                for j in range(PARITIES):
                     merge(widest, j)
-                if step == last_bank[middle] + CONV_LAG[middle]:
-                    convolve(middle, j)
         convolve(narrowest, 0)
         for b in range(SLABS_PER_BANK):
             quantise(n_banks - 1, (b, b + 1))

@@ -24,12 +24,10 @@ PAIRS = FEATURES // 2
 HALVES = PAIRS // P
 SLABS_PER_BANK = 2
 SLAB_COLS = P * PACK
-WARM_PASSES = 12
 BANKS_BEFORE_BIASES = 5
 BLOCK = 32
 SPREAD = P // BLOCK
-CONV_LAG = 2
-MERGE_STEP = 6
+BIAS_STEP = 6
 
 assert TOKENS == P and FEATURES == P * PACK
 
@@ -72,23 +70,6 @@ def tile_textheading_pa_s_kernel(tc, words_emb, W2, b2, W3, b3, W4, b4, out):
                 if len(w_rows) == BANKS_BEFORE_BIASES:
                     load_biases()
 
-        zeros = keep.tile([P, P * PACK], BF16, align_bytes=64)
-        zero_codes = keep.tile([P, P], U32, align_bytes=64)
-        zero_scales = keep.tile([P, P], U8, align_bytes=64)
-        nc.vector.memset(zeros[:].bitcast(F32), 0.0)
-        nc.vector.quantize_mx(out=zero_codes[:].bitcast(FP8X4), scales=zero_scales[:], in_=zeros[:])
-        idle_sums = flip.tile([P, P], F32, name="idle_sums", tag="flipped")
-        for i in range(WARM_PASSES):
-            nc.tensor.matmul_mx(
-                out=idle_sums[:],
-                lhsT=zero_codes[:].bitcast(FP8X4),
-                lhsT_scale=zero_scales[:],
-                rhs=zero_codes[:].bitcast(FP8X4),
-                rhs_scale=zero_scales[:],
-                start=True,
-                stop=True,
-            )
-
         identity = keep.tile([P, P], F32)
         make_identity(nc, identity[:])
         ones = keep.tile([P, 1], F32)
@@ -112,15 +93,12 @@ def tile_textheading_pa_s_kernel(tc, words_emb, W2, b2, W3, b3, W4, b4, out):
         x_scales = keep.tile([P, SHIFTS * TOKENS], U8, align_bytes=64)
         x_pairs = x_grouped[:].bitcast(F32).rearrange("p (s t u) -> p s t u", s=SHIFTS, u=HALVES)
         nc.vector.memset(x_pairs[:, 1:, TOKENS - SHIFTS + 1 :, :], 0.0)
-        x_flipped = []
-        for copy in (nc.vector.tensor_copy, nc.scalar.copy):
-            flipped = flip.tile([P, SLABS_PER_BANK * HALVES, P], F32, name="x_flipped", tag="flipped")
-            for u in range(HALVES):
-                nc.tensor.transpose(flipped[:, u, :], x_rows[:].bitcast(F32)[:, u::HALVES], identity[:])
-            x_flipped.append((copy, flipped))
-        for s in range(SHIFTS):
-            copy, flipped = x_flipped[s % len(x_flipped)]
-            copy(out=x_pairs[:, s, : TOKENS - s, :], in_=flipped[:, 0:HALVES, s:].rearrange("p u t -> p t u"))
+        x_flipped = flip.tile([P, SLABS_PER_BANK * HALVES, P], F32, name="x_flipped", tag="flipped")
+        for u in range(HALVES):
+            nc.tensor.transpose(x_flipped[:, u, :], x_rows[:].bitcast(F32)[:, u::HALVES], identity[:])
+        nc.vector.tensor_copy(out=x_pairs[:, 0, :, :], in_=x_flipped[:, 0:HALVES, :].rearrange("p u t -> p t u"))
+        for s in range(1, SHIFTS):
+            nc.vector.tensor_copy(out=x_pairs[:, s, : TOKENS - s, :], in_=x_pairs[:, 0, s:, :])
         nc.vector.quantize_mx(out=x_codes[:].bitcast(FP8X4), scales=x_scales[:], in_=x_grouped[:])
 
         n_banks = n_slabs // SLABS_PER_BANK
@@ -191,46 +169,42 @@ def tile_textheading_pa_s_kernel(tc, words_emb, W2, b2, W3, b3, W4, b4, out):
                     stop=(k == width - 1),
                 )
 
-        def merge(width, j):
+        def operands(width, j):
             positions = WORDS - width + 1
             column = WIDTHS.index(width) * PARITIES + j
+            source = by_text(conv[width][:, j, :], positions)
+            return by_text(code[j][:], positions), source, bias[:, column : column + 1]
+
+        def start(width, j):
+            target, source, column = operands(width, j)
+            nc.scalar.activation(out=target, in_=source, func=ACT.Relu, bias=column)
+
+        def merge(width, j):
+            target, source, column = operands(width, j)
             nc.vector.scalar_tensor_tensor(
-                out=by_text(code[j][:], positions),
-                in0=by_text(conv[width][:, j, :], positions),
-                scalar=bias[:, column : column + 1],
-                in1=by_text(code[j][:], positions),
-                op0=ALU.add,
-                op1=ALU.max,
+                out=target, in0=source, scalar=column, in1=target, op0=ALU.add, op1=ALU.max
             )
 
-        widest, middle, narrowest = WIDTHS
-        due = {}
-        for width in WIDTHS:
-            for j in range(PARITIES):
-                last_slab = first_slab[width] + (j + 1) * width - 1
-                due[width, j] = last_slab // SLABS_PER_BANK + CONV_LAG
         for step in range(n_banks):
             if step < n_banks - 1:
                 transpose(step)
             else:
                 transpose_in_halves(step)
-            if step == MERGE_STEP - 1:
+            if step == BIAS_STEP:
                 turn_biases()
             if step >= 1:
                 quantise(step - 1)
-            for width in (widest, middle):
-                for j in range(PARITIES):
-                    if step == due[width, j]:
-                        convolve(width, j)
-            if step == MERGE_STEP:
-                for j in range(PARITIES):
-                    merge(widest, j)
-        convolve(narrowest, 0)
         for b in range(SLABS_PER_BANK):
             quantise(n_banks - 1, (b, b + 1))
-        convolve(narrowest, 1)
+        widest, middle, narrowest = WIDTHS
+        for width in WIDTHS:
+            for j in range(PARITIES):
+                convolve(width, j)
+        for j in range(PARITIES):
+            start(widest, j)
         for j in range(PARITIES):
             merge(middle, j)
+        for j in range(PARITIES):
             merge(narrowest, j)
 
         blocks = keep.tile([P, PARITIES, P], F32, align_bytes=64)

@@ -27,6 +27,9 @@ SLAB_COLS = P * PACK
 BANKS_BEFORE_BIASES = 5
 BLOCK = 32
 SPREAD = P // BLOCK
+WARM_PASSES = 10
+VECTOR_EMPTIES = 5
+FIRST_CONV_STEP = 4
 BIAS_STEP = 6
 
 assert TOKENS == P and FEATURES == P * PACK
@@ -50,6 +53,23 @@ def tile_textheading_pa_s_kernel(tc, words_emb, W2, b2, W3, b3, W4, b4, out):
         flip = ctx.enter_context(tc.psum_pool(name="flip", bufs=5))
         sums = ctx.enter_context(tc.psum_pool(name="sums", bufs=1))
         ctx.enter_context(tc.manual_schedule())
+
+        zeros = keep.tile([P, P * PACK], BF16, align_bytes=64)
+        zero_codes = keep.tile([P, P], U32, align_bytes=64)
+        zero_scales = keep.tile([P, P], U8, align_bytes=64)
+        nc.vector.memset(zeros[:].bitcast(F32), 0.0)
+        nc.vector.quantize_mx(out=zero_codes[:].bitcast(FP8X4), scales=zero_scales[:], in_=zeros[:])
+        idle_sums = flip.tile([P, P], F32, name="idle_sums", tag="flipped")
+        for i in range(WARM_PASSES):
+            nc.tensor.matmul_mx(
+                out=idle_sums[:],
+                lhsT=zero_codes[:].bitcast(FP8X4),
+                lhsT_scale=zero_scales[:],
+                rhs=zero_codes[:].bitcast(FP8X4),
+                rhs_scale=zero_scales[:],
+                start=True,
+                stop=True,
+            )
 
         x_rows = keep.tile([P, FEATURES], BF16)
         nc.sync.dma_start(out=x_rows[:], in_=words_emb.rearrange("n t d -> (n t) d"))
@@ -115,7 +135,8 @@ def tile_textheading_pa_s_kernel(tc, words_emb, W2, b2, W3, b3, W4, b4, out):
             for b in range(SLABS_PER_BANK):
                 transpose_slab(bank, b, flipped[:, b * HALVES : (b + 1) * HALVES, :])
             pairs = w_grouped[bank][:].bitcast(F32).rearrange("p (b q u) -> p b q u", b=SLABS_PER_BANK, u=HALVES)
-            nc.scalar.copy(out=pairs, in_=flipped[:].rearrange("p (b u) q -> p b q u", u=HALVES))
+            copy = nc.vector.tensor_copy if bank == VECTOR_EMPTIES else nc.scalar.copy
+            copy(out=pairs, in_=flipped[:].rearrange("p (b u) q -> p b q u", u=HALVES))
 
         def transpose_slab(bank, b, flipped):
             words = w_rows[bank][:].bitcast(F32)
@@ -185,6 +206,7 @@ def tile_textheading_pa_s_kernel(tc, words_emb, W2, b2, W3, b3, W4, b4, out):
                 out=target, in0=source, scalar=column, in1=target, op0=ALU.add, op1=ALU.max
             )
 
+        widest, middle, narrowest = WIDTHS
         for step in range(n_banks):
             if step < n_banks - 1:
                 transpose(step)
@@ -194,10 +216,12 @@ def tile_textheading_pa_s_kernel(tc, words_emb, W2, b2, W3, b3, W4, b4, out):
                 turn_biases()
             if step >= 1:
                 quantise(step - 1)
+            if step == FIRST_CONV_STEP:
+                convolve(widest, 0)
         for b in range(SLABS_PER_BANK):
             quantise(n_banks - 1, (b, b + 1))
-        widest, middle, narrowest = WIDTHS
-        for width in WIDTHS:
+        convolve(widest, 1)
+        for width in (middle, narrowest):
             for j in range(PARITIES):
                 convolve(width, j)
         for j in range(PARITIES):
@@ -214,13 +238,14 @@ def tile_textheading_pa_s_kernel(tc, words_emb, W2, b2, W3, b3, W4, b4, out):
             square_sum.append(keep.tile([P, 1], F32, name="square_sum%d" % j))
         for j in range(PARITIES):
             turned_for_scalar = flip.tile([P, P], F32, name="turned_for_scalar", tag="flipped")
-            turned_for_vector = flip.tile([P, P], F32, name="turned_for_vector", tag="flipped")
-            for turned in (turned_for_scalar, turned_for_vector):
-                nc.tensor.transpose(turned[:], code[j][:], permutation[:])
-            nc.vector.transpose(blocks[:, j, :], turned_for_vector[:])
+            nc.tensor.transpose(turned_for_scalar[:], code[j][:], permutation[:])
             nc.scalar.activation(
                 out=squares[:, j, :], in_=turned_for_scalar[:], func=ACT.Square, accum_out=square_sum[j][:]
             )
+        for j in range(PARITIES):
+            turned_for_vector = flip.tile([P, P], F32, name="turned_for_vector", tag="flipped")
+            nc.tensor.transpose(turned_for_vector[:], code[j][:], permutation[:])
+            nc.vector.transpose(blocks[:, j, :], turned_for_vector[:])
         inverse_norm = keep.tile([P, BLOCK], F32, align_bytes=64)
         nc.scalar.activation(
             out=inverse_norm[:],

@@ -30,6 +30,7 @@ SPREAD = P // BLOCK
 WARM_PASSES = 10
 VECTOR_EMPTIES = 5
 FIRST_CONV_STEP = 4
+EARLY_OFFSETS = 2
 BIAS_STEP = 6
 
 assert TOKENS == P and FEATURES == P * PACK
@@ -85,8 +86,13 @@ def tile_textheading_pa_s_kernel(tc, words_emb, W2, b2, W3, b3, W4, b4, out):
             runs = weights[width].rearrange("(q j) k d -> q (j k d)", j=PARITIES)
             for first in range(0, PARITIES * width * FEATURES, SLABS_PER_BANK * FEATURES):
                 rows = keep.tile([P, SLABS_PER_BANK * FEATURES], BF16, name="w_rows%d" % len(w_rows))
-                nc.sync.dma_start(out=rows[:], in_=runs[:, first : first + SLABS_PER_BANK * FEATURES])
                 w_rows.append(rows)
+                pieces = SLABS_PER_BANK if len(w_rows) == n_slabs // SLABS_PER_BANK else 1
+                size = SLABS_PER_BANK * FEATURES // pieces
+                for piece in range(0, SLABS_PER_BANK * FEATURES, size):
+                    nc.sync.dma_start(
+                        out=rows[:, piece : piece + size], in_=runs[:, first + piece : first + piece + size]
+                    )
                 if len(w_rows) == BANKS_BEFORE_BIASES:
                     load_biases()
 
@@ -144,7 +150,7 @@ def tile_textheading_pa_s_kernel(tc, words_emb, W2, b2, W3, b3, W4, b4, out):
                 nc.tensor.transpose(flipped[:, u, :], words[:, b * PAIRS + u : (b + 1) * PAIRS : HALVES], identity[:])
 
         def transpose_in_halves(bank):
-            for b, copy in enumerate((nc.scalar.copy, nc.vector.tensor_copy)):
+            for b, copy in enumerate((nc.vector.tensor_copy, nc.scalar.copy)):
                 flipped = flip.tile([P, SLABS_PER_BANK * HALVES, P], F32, name="half", tag="flipped")
                 transpose_slab(bank, b, flipped[:, 0:HALVES, :])
                 pairs = w_grouped[bank][:, b * SLAB_COLS : (b + 1) * SLAB_COLS].bitcast(F32)
@@ -175,8 +181,8 @@ def tile_textheading_pa_s_kernel(tc, words_emb, W2, b2, W3, b3, W4, b4, out):
         for width in WIDTHS:
             conv[width] = sums.tile([P, PARITIES, TOKENS], F32, name="conv%d" % width)
 
-        def convolve(width, j):
-            for k in range(width):
+        def convolve(width, j, offsets=None):
+            for k in offsets or range(width):
                 bank, place = divmod(first_slab[width] + j * width + k, SLABS_PER_BANK)
                 slab = slice(place * P, (place + 1) * P)
                 shifted = slice(k * TOKENS, (k + 1) * TOKENS)
@@ -218,9 +224,10 @@ def tile_textheading_pa_s_kernel(tc, words_emb, W2, b2, W3, b3, W4, b4, out):
                 quantise(step - 1)
             if step == FIRST_CONV_STEP:
                 convolve(widest, 0)
+                convolve(widest, 1, range(0, EARLY_OFFSETS))
         for b in range(SLABS_PER_BANK):
             quantise(n_banks - 1, (b, b + 1))
-        convolve(widest, 1)
+        convolve(widest, 1, range(EARLY_OFFSETS, widest))
         for width in (middle, narrowest):
             for j in range(PARITIES):
                 convolve(width, j)
@@ -231,7 +238,7 @@ def tile_textheading_pa_s_kernel(tc, words_emb, W2, b2, W3, b3, W4, b4, out):
         for j in range(PARITIES):
             merge(narrowest, j)
 
-        blocks = keep.tile([P, PARITIES, P], F32, align_bytes=64)
+        blocks = keep.tile([P, PARITIES * P], F32, align_bytes=64)
         squares = keep.tile([P, PARITIES, P], F32)
         square_sum = []
         for j in range(PARITIES):
@@ -242,10 +249,12 @@ def tile_textheading_pa_s_kernel(tc, words_emb, W2, b2, W3, b3, W4, b4, out):
             nc.scalar.activation(
                 out=squares[:, j, :], in_=turned_for_scalar[:], func=ACT.Square, accum_out=square_sum[j][:]
             )
+        turned_for_vector = flip.tile([P, SPREAD, PARITIES, BLOCK], F32, name="turned_for_vector", tag="flipped")
         for j in range(PARITIES):
-            turned_for_vector = flip.tile([P, P], F32, name="turned_for_vector", tag="flipped")
-            nc.tensor.transpose(turned_for_vector[:], code[j][:], permutation[:])
-            nc.vector.transpose(blocks[:, j, :], turned_for_vector[:])
+            nc.tensor.transpose(turned_for_vector[:, :, j, :], code[j][:], permutation[:])
+        for half in range(PARITIES):
+            columns = slice(half * P, (half + 1) * P)
+            nc.vector.transpose(blocks[:, columns], turned_for_vector[:].rearrange("t c j i -> t (c j i)")[:, columns])
         inverse_norm = keep.tile([P, BLOCK], F32, align_bytes=64)
         nc.scalar.activation(
             out=inverse_norm[:],
@@ -255,17 +264,16 @@ def tile_textheading_pa_s_kernel(tc, words_emb, W2, b2, W3, b3, W4, b4, out):
         )
         inverse_by_position = keep.tile([P, BLOCK], F32, align_bytes=64)
         nc.vector.transpose(inverse_by_position[:], inverse_norm[:])
-        result = keep.tile([P, SPREAD, PARITIES, POSITIONS], F32)
-        for j in range(PARITIES):
-            nc.vector.scalar_tensor_tensor(
-                out=result[:, :, j, :],
-                in0=inverse_by_position[:, :POSITIONS].unsqueeze(1).to_broadcast([P, SPREAD, POSITIONS]),
-                scalar=1.0 / EPS,
-                in1=blocks[:, j, :].rearrange("q (c p) -> q c p", p=BLOCK)[:, :, :POSITIONS],
-                op0=ALU.min,
-                op1=ALU.mult,
-            )
+        result = keep.tile([P, SPREAD * PARITIES, POSITIONS], F32)
+        nc.vector.scalar_tensor_tensor(
+            out=result[:],
+            in0=inverse_by_position[:, :POSITIONS].unsqueeze(1).to_broadcast([P, SPREAD * PARITIES, POSITIONS]),
+            scalar=1.0 / EPS,
+            in1=blocks[:].rearrange("q (b p) -> q b p", p=BLOCK)[:, :, :POSITIONS],
+            op0=ALU.min,
+            op1=ALU.mult,
+        )
         nc.sync.dma_start(
             out=out.rearrange("n (i b) p -> (n i) (b p)", i=BLOCK),
-            in_=result[:].rearrange("q c j p -> q (c j p)"),
+            in_=result[:].rearrange("q b p -> q (b p)"),
         )

@@ -29,8 +29,9 @@ BLOCK = 32
 SPREAD = P // BLOCK
 WARM_PASSES = 10
 VECTOR_EMPTIES = 5
+SORTED_BANK = 5
 FIRST_CONV_STEP = 4
-EARLY_OFFSETS = 2
+IDLE_PASSES = 2
 BIAS_STEP = 6
 
 assert TOKENS == P and FEATURES == P * PACK
@@ -60,17 +61,21 @@ def tile_textheading_pa_s_kernel(tc, words_emb, W2, b2, W3, b3, W4, b4, out):
         zero_scales = keep.tile([P, P], U8, align_bytes=64)
         nc.vector.memset(zeros[:].bitcast(F32), 0.0)
         nc.vector.quantize_mx(out=zero_codes[:].bitcast(FP8X4), scales=zero_scales[:], in_=zeros[:])
-        idle_sums = flip.tile([P, P], F32, name="idle_sums", tag="flipped")
-        for i in range(WARM_PASSES):
-            nc.tensor.matmul_mx(
-                out=idle_sums[:],
-                lhsT=zero_codes[:].bitcast(FP8X4),
-                lhsT_scale=zero_scales[:],
-                rhs=zero_codes[:].bitcast(FP8X4),
-                rhs_scale=zero_scales[:],
-                start=True,
-                stop=True,
-            )
+
+        def idle_passes(count):
+            idle_sums = flip.tile([P, P], F32, name="idle_sums", tag="flipped")
+            for i in range(count):
+                nc.tensor.matmul_mx(
+                    out=idle_sums[:],
+                    lhsT=zero_codes[:].bitcast(FP8X4),
+                    lhsT_scale=zero_scales[:],
+                    rhs=zero_codes[:].bitcast(FP8X4),
+                    rhs_scale=zero_scales[:],
+                    start=True,
+                    stop=True,
+                )
+
+        idle_passes(WARM_PASSES)
 
         x_rows = keep.tile([P, FEATURES], BF16)
         nc.sync.dma_start(out=x_rows[:], in_=words_emb.rearrange("n t d -> (n t) d"))
@@ -122,10 +127,19 @@ def tile_textheading_pa_s_kernel(tc, words_emb, W2, b2, W3, b3, W4, b4, out):
         x_flipped = flip.tile([P, SLABS_PER_BANK * HALVES, P], F32, name="x_flipped", tag="flipped")
         for u in range(HALVES):
             nc.tensor.transpose(x_flipped[:, u, :], x_rows[:].bitcast(F32)[:, u::HALVES], identity[:])
-        nc.vector.tensor_copy(out=x_pairs[:, 0, :, :], in_=x_flipped[:, 0:HALVES, :].rearrange("p u t -> p t u"))
-        for s in range(1, SHIFTS):
-            nc.vector.tensor_copy(out=x_pairs[:, s, : TOKENS - s, :], in_=x_pairs[:, 0, s:, :])
-        nc.vector.quantize_mx(out=x_codes[:].bitcast(FP8X4), scales=x_scales[:], in_=x_grouped[:])
+        for s in range(SHIFTS):
+            if s < SHIFTS // 2:
+                source = x_flipped[:, 0:HALVES, s:].rearrange("p u t -> p t u")
+            else:
+                source = x_pairs[:, 0, s:, :]
+            nc.vector.tensor_copy(out=x_pairs[:, s, : TOKENS - s, :], in_=source)
+        for half in range(2):
+            columns = slice(half * SHIFTS // 2 * TOKENS, (half + 1) * SHIFTS // 2 * TOKENS)
+            nc.vector.quantize_mx(
+                out=x_codes[:, columns].bitcast(FP8X4),
+                scales=x_scales[:, columns],
+                in_=x_grouped[:, columns.start * PACK : columns.stop * PACK],
+            )
 
         n_banks = n_slabs // SLABS_PER_BANK
         w_grouped = []
@@ -147,7 +161,19 @@ def tile_textheading_pa_s_kernel(tc, words_emb, W2, b2, W3, b3, W4, b4, out):
         def transpose_slab(bank, b, flipped):
             words = w_rows[bank][:].bitcast(F32)
             for u in range(HALVES):
-                nc.tensor.transpose(flipped[:, u, :], words[:, b * PAIRS + u : (b + 1) * PAIRS : HALVES], identity[:])
+                if bank == SORTED_BANK:
+                    half = sorted_words[:, b, u, :]
+                else:
+                    half = words[:, b * PAIRS + u : (b + 1) * PAIRS : HALVES]
+                nc.tensor.transpose(flipped[:, u, :], half, identity[:])
+
+        sorted_words = keep.tile([P, SLABS_PER_BANK, HALVES, P], F32)
+
+        def sort_words(bank):
+            words = w_rows[bank][:].bitcast(F32)
+            nc.vector.tensor_copy(
+                out=sorted_words[:], in_=words.rearrange("p (b w u) -> p b u w", b=SLABS_PER_BANK, u=HALVES)
+            )
 
         def transpose_in_halves(bank):
             for b, copy in enumerate((nc.vector.tensor_copy, nc.scalar.copy)):
@@ -181,8 +207,8 @@ def tile_textheading_pa_s_kernel(tc, words_emb, W2, b2, W3, b3, W4, b4, out):
         for width in WIDTHS:
             conv[width] = sums.tile([P, PARITIES, TOKENS], F32, name="conv%d" % width)
 
-        def convolve(width, j, offsets=None):
-            for k in offsets or range(width):
+        def convolve(width, j):
+            for k in range(width):
                 bank, place = divmod(first_slab[width] + j * width + k, SLABS_PER_BANK)
                 slab = slice(place * P, (place + 1) * P)
                 shifted = slice(k * TOKENS, (k + 1) * TOKENS)
@@ -222,12 +248,14 @@ def tile_textheading_pa_s_kernel(tc, words_emb, W2, b2, W3, b3, W4, b4, out):
                 turn_biases()
             if step >= 1:
                 quantise(step - 1)
+            if step == SORTED_BANK - 2:
+                sort_words(SORTED_BANK)
             if step == FIRST_CONV_STEP:
                 convolve(widest, 0)
-                convolve(widest, 1, range(0, EARLY_OFFSETS))
+                idle_passes(IDLE_PASSES)
         for b in range(SLABS_PER_BANK):
             quantise(n_banks - 1, (b, b + 1))
-        convolve(widest, 1, range(EARLY_OFFSETS, widest))
+        convolve(widest, 1)
         for width in (middle, narrowest):
             for j in range(PARITIES):
                 convolve(width, j)

from contextlib import ExitStack

import concourse.mybir as mybir
from concourse.masks import make_identity

F32 = mybir.dt.float32
BF16 = mybir.dt.bfloat16
U32 = mybir.dt.uint32
U8 = mybir.dt.uint8
FP8X4 = mybir.dt.float8_e4m3fn_x4
ALU = mybir.AluOpType
ACT = mybir.ActivationFunctionType

P = 128
PACK = 4
TEXTS, WORDS, FEATURES, FILTERS = 4, 32, 512, 256
TOKENS = TEXTS * WORDS
WIDTHS = (4, 3, 2)
SHIFTS = max(WIDTHS)
PARITIES = FILTERS // P
POSITIONS = WORDS - min(WIDTHS) + 1
EPS = 1e-12
PAIRS = FEATURES // 2
HALVES = PAIRS // P
SLABS_PER_BANK = 2
SLAB_COLS = P * PACK
BANKS_BEFORE_BIASES = 5
BLOCK = 32
SPREAD = P // BLOCK
WARM_PASSES = 10
VECTOR_EMPTIES = 5
SORTED_BANK = 5
FIRST_CONV_STEP = 4
IDLE_PASSES = 2
BIAS_STEP = 6

assert TOKENS == P and FEATURES == P * PACK

FLOPS = 2 * FEATURES * FILTERS * TEXTS * sum(w * (WORDS - w + 1) for w in WIDTHS)


def tile_textheading_pa_s_kernel(tc, words_emb, W2, b2, W3, b3, W4, b4, out):
    nc = tc.nc
    weights = {2: W2, 3: W3, 4: W4}
    biases = {2: b2, 3: b3, 4: b4}

    first_slab = {}
    n_slabs = 0
    for width in WIDTHS:
        first_slab[width] = n_slabs
        n_slabs += PARITIES * width

    with ExitStack() as ctx:
        keep = ctx.enter_context(tc.tile_pool(name="keep", bufs=1))
        flip = ctx.enter_context(tc.psum_pool(name="flip", bufs=5))
        sums = ctx.enter_context(tc.psum_pool(name="sums", bufs=1))
        ctx.enter_context(tc.manual_schedule())

        zeros = keep.tile([P, P * PACK], BF16, align_bytes=64)
        zero_codes = keep.tile([P, P], U32, align_bytes=64)
        zero_scales = keep.tile([P, P], U8, align_bytes=64)
        nc.vector.memset(zeros[:].bitcast(F32), 0.0)
        nc.vector.quantize_mx(out=zero_codes[:].bitcast(FP8X4), scales=zero_scales[:], in_=zeros[:])

        def idle_passes(count):
            idle_sums = flip.tile([P, P], F32, name="idle_sums", tag="flipped")
            for i in range(count):
                nc.tensor.matmul_mx(
                    out=idle_sums[:],
                    lhsT=zero_codes[:].bitcast(FP8X4),
                    lhsT_scale=zero_scales[:],
                    rhs=zero_codes[:].bitcast(FP8X4),
                    rhs_scale=zero_scales[:],
                    start=True,
                    stop=True,
                )

        idle_passes(WARM_PASSES)

        x_rows = keep.tile([P, FEATURES], BF16)
        nc.sync.dma_start(out=x_rows[:], in_=words_emb.rearrange("n t d -> (n t) d"))
        b_rows = keep.tile([P, FILTERS], BF16)
        nc.vector.memset(b_rows[:].bitcast(F32), 0.0)

        def load_biases():
            for i, width in enumerate(WIDTHS):
                nc.sync.dma_start(out=b_rows[i : i + 1, :], in_=biases[width].rearrange("(o f) -> o f", o=1))

        w_rows = []
        for width in WIDTHS:
            runs = weights[width].rearrange("(q j) k d -> q (j k d)", j=PARITIES)
            for first in range(0, PARITIES * width * FEATURES, SLABS_PER_BANK * FEATURES):
                rows = keep.tile([P, SLABS_PER_BANK * FEATURES], BF16, name="w_rows%d" % len(w_rows))
                w_rows.append(rows)
                pieces = SLABS_PER_BANK if len(w_rows) == n_slabs // SLABS_PER_BANK else 1
                size = SLABS_PER_BANK * FEATURES // pieces
                for piece in range(0, SLABS_PER_BANK * FEATURES, size):
                    nc.sync.dma_start(
                        out=rows[:, piece : piece + size], in_=runs[:, first + piece : first + piece + size]
                    )
                if len(w_rows) == BANKS_BEFORE_BIASES:
                    load_biases()

        identity = keep.tile([P, P], F32)
        make_identity(nc, identity[:])
        ones = keep.tile([P, 1], F32)
        nc.vector.memset(ones[:], 1.0)
        permutation = keep.tile([P, P], F32)
        nc.gpsimd.tensor_copy(
            out=permutation[:].rearrange("p (c i) -> p c i", c=SPREAD),
            in_=identity[:].rearrange("p (i c) -> p c i", c=SPREAD),
        )
        code = []
        for j in range(PARITIES):
            code.append(keep.tile([P, TOKENS], F32, name="code%d" % j))
            nc.vector.memset(code[j][:], 0.0)
        for j in range(PARITIES):
            nc.vector.memset(code[j][:].rearrange("q (n p) -> q n p", p=WORDS)[:, :, POSITIONS:], 1.0)
        table_warmer = keep.tile([P, 1], F32)
        nc.scalar.activation(out=table_warmer[:], in_=ones[:], func=ACT.Abs_reciprocal_sqrt)

        x_grouped = keep.tile([P, SHIFTS * TOKENS * PACK], BF16, align_bytes=64)
        x_codes = keep.tile([P, SHIFTS * TOKENS], U32, align_bytes=64)
        x_scales = keep.tile([P, SHIFTS * TOKENS], U8, align_bytes=64)
        x_pairs = x_grouped[:].bitcast(F32).rearrange("p (s t u) -> p s t u", s=SHIFTS, u=HALVES)
        nc.vector.memset(x_pairs[:, 1:, TOKENS - SHIFTS + 1 :, :], 0.0)
        x_flipped = flip.tile([P, SLABS_PER_BANK * HALVES, P], F32, name="x_flipped", tag="flipped")
        for u in range(HALVES):
            nc.tensor.transpose(x_flipped[:, u, :], x_rows[:].bitcast(F32)[:, u::HALVES], identity[:])
        for s in range(SHIFTS):
            if s < SHIFTS // 2:
                source = x_flipped[:, 0:HALVES, s:].rearrange("p u t -> p t u")
            else:
                source = x_pairs[:, 0, s:, :]
            nc.vector.tensor_copy(out=x_pairs[:, s, : TOKENS - s, :], in_=source)
        for half in range(2):
            columns = slice(half * SHIFTS // 2 * TOKENS, (half + 1) * SHIFTS // 2 * TOKENS)
            nc.vector.quantize_mx(
                out=x_codes[:, columns].bitcast(FP8X4),
                scales=x_scales[:, columns],
                in_=x_grouped[:, columns.start * PACK : columns.stop * PACK],
            )

        n_banks = n_slabs // SLABS_PER_BANK
        w_grouped = []
        w_codes = []
        w_scales = []
        for bank in range(n_banks):
            w_grouped.append(keep.tile([P, SLABS_PER_BANK * SLAB_COLS], BF16, name="w_grouped%d" % bank, align_bytes=64))
            w_codes.append(keep.tile([P, SLABS_PER_BANK * P], U32, name="w_codes%d" % bank, align_bytes=64))
            w_scales.append(keep.tile([P, SLABS_PER_BANK * P], U8, name="w_scales%d" % bank, align_bytes=64))

        def transpose(bank):
            flipped = flip.tile([P, SLABS_PER_BANK * HALVES, P], F32, name="flipped", tag="flipped")
            for b in range(SLABS_PER_BANK):
                transpose_slab(bank, b, flipped[:, b * HALVES : (b + 1) * HALVES, :])
            pairs = w_grouped[bank][:].bitcast(F32).rearrange("p (b q u) -> p b q u", b=SLABS_PER_BANK, u=HALVES)
            copy = nc.vector.tensor_copy if bank == VECTOR_EMPTIES else nc.scalar.copy
            copy(out=pairs, in_=flipped[:].rearrange("p (b u) q -> p b q u", u=HALVES))

        def transpose_slab(bank, b, flipped):
            words = w_rows[bank][:].bitcast(F32)
            for u in range(HALVES):
                if bank == SORTED_BANK:
                    half = sorted_words[:, b, u, :]
                else:
                    half = words[:, b * PAIRS + u : (b + 1) * PAIRS : HALVES]
                nc.tensor.transpose(flipped[:, u, :], half, identity[:])

        sorted_words = keep.tile([P, SLABS_PER_BANK, HALVES, P], F32)

        def sort_words(bank):
            words = w_rows[bank][:].bitcast(F32)
            nc.vector.tensor_copy(
                out=sorted_words[:], in_=words.rearrange("p (b w u) -> p b u w", b=SLABS_PER_BANK, u=HALVES)
            )

        def transpose_in_halves(bank):
            for b, copy in enumerate((nc.vector.tensor_copy, nc.scalar.copy)):
                flipped = flip.tile([P, SLABS_PER_BANK * HALVES, P], F32, name="half", tag="flipped")
                transpose_slab(bank, b, flipped[:, 0:HALVES, :])
                pairs = w_grouped[bank][:, b * SLAB_COLS : (b + 1) * SLAB_COLS].bitcast(F32)
                copy(
                    out=pairs.rearrange("p (q u) -> p q u", u=HALVES),
                    in_=flipped[:, 0:HALVES, :].rearrange("p u q -> p q u"),
                )

        def quantise(bank, slabs=(0, SLABS_PER_BANK)):
            first, end = slabs
            nc.vector.quantize_mx(
                out=w_codes[bank][:, first * P : end * P].bitcast(FP8X4),
                scales=w_scales[bank][:, first * P : end * P],
                in_=w_grouped[bank][:, first * SLAB_COLS : end * SLAB_COLS],
            )

        bias = keep.tile([P, len(WIDTHS) * PARITIES], F32)

        def turn_biases():
            b_flipped = flip.tile([P, SLABS_PER_BANK * HALVES, P], F32, name="b_flipped", tag="flipped")
            nc.tensor.transpose(b_flipped[:, 0, :], b_rows[:].bitcast(F32), identity[:])
            nc.vector.tensor_copy(out=bias[:], in_=b_flipped[:, 0, 0 : len(WIDTHS)].bitcast(BF16))

        def by_text(ap, positions):
            return ap.rearrange("q (n p) -> q n p", p=WORDS)[:, :, :positions]

        conv = {}
        for width in WIDTHS:
            conv[width] = sums.tile([P, PARITIES, TOKENS], F32, name="conv%d" % width)

        def convolve(width, j):
            for k in range(width):
                bank, place = divmod(first_slab[width] + j * width + k, SLABS_PER_BANK)
                slab = slice(place * P, (place + 1) * P)
                shifted = slice(k * TOKENS, (k + 1) * TOKENS)
                nc.tensor.matmul_mx(
                    out=conv[width][:, j, :],
                    lhsT=w_codes[bank][:, slab].bitcast(FP8X4),
                    lhsT_scale=w_scales[bank][:, slab],
                    rhs=x_codes[:, shifted].bitcast(FP8X4),
                    rhs_scale=x_scales[:, shifted],
                    start=(k == 0),
                    stop=(k == width - 1),
                )

        def operands(width, j):
            positions = WORDS - width + 1
            column = WIDTHS.index(width) * PARITIES + j
            source = by_text(conv[width][:, j, :], positions)
            return by_text(code[j][:], positions), source, bias[:, column : column + 1]

        def start(width, j):
            target, source, column = operands(width, j)
            nc.scalar.activation(out=target, in_=source, func=ACT.Relu, bias=column)

        def merge(width, j):
            target, source, column = operands(width, j)
            nc.vector.scalar_tensor_tensor(
                out=target, in0=source, scalar=column, in1=target, op0=ALU.add, op1=ALU.max
            )

        widest, middle, narrowest = WIDTHS
        for step in range(n_banks):
            if step < n_banks - 1:
                transpose(step)
            else:
                transpose_in_halves(step)
            if step == BIAS_STEP:
                turn_biases()
            if step >= 1:
                quantise(step - 1)
            if step == SORTED_BANK - 2:
                sort_words(SORTED_BANK)
            if step == FIRST_CONV_STEP:
                convolve(widest, 0)
                idle_passes(IDLE_PASSES)
        for b in range(SLABS_PER_BANK):
            quantise(n_banks - 1, (b, b + 1))
        convolve(widest, 1)
        for width in (middle, narrowest):
            for j in range(PARITIES):
                convolve(width, j)
        for j in range(PARITIES):
            start(widest, j)
        for j in range(PARITIES):
            merge(middle, j)
        for j in range(PARITIES):
            merge(narrowest, j)

        blocks = keep.tile([P, PARITIES * P], F32, align_bytes=64)
        squares = keep.tile([P, PARITIES, P], F32)
        square_sum = []
        for j in range(PARITIES):
            square_sum.append(keep.tile([P, 1], F32, name="square_sum%d" % j))
        for j in range(PARITIES):
            turned_for_scalar = flip.tile([P, P], F32, name="turned_for_scalar", tag="flipped")
            nc.tensor.transpose(turned_for_scalar[:], code[j][:], permutation[:])
            nc.scalar.activation(
                out=squares[:, j, :], in_=turned_for_scalar[:], func=ACT.Square, accum_out=square_sum[j][:]
            )
        turned_for_vector = flip.tile([P, SPREAD, PARITIES, BLOCK], F32, name="turned_for_vector", tag="flipped")
        for j in range(PARITIES):
            nc.tensor.transpose(turned_for_vector[:, :, j, :], code[j][:], permutation[:])
        for half in range(PARITIES):
            columns = slice(half * P, (half + 1) * P)
            nc.vector.transpose(blocks[:, columns], turned_for_vector[:].rearrange("t c j i -> t (c j i)")[:, columns])
        inverse_norm = keep.tile([P, BLOCK], F32, align_bytes=64)
        nc.scalar.activation(
            out=inverse_norm[:],
            in_=square_sum[1][:].to_broadcast([P, BLOCK]),
            func=ACT.Abs_reciprocal_sqrt,
            bias=square_sum[0][:],
        )
        inverse_by_position = keep.tile([P, BLOCK], F32, align_bytes=64)
        nc.vector.transpose(inverse_by_position[:], inverse_norm[:])
        result = keep.tile([P, SPREAD * PARITIES, POSITIONS], F32)
        nc.vector.scalar_tensor_tensor(
            out=result[:],
            in0=inverse_by_position[:, :POSITIONS].unsqueeze(1).to_broadcast([P, SPREAD * PARITIES, POSITIONS]),
            scalar=1.0 / EPS,
            in1=blocks[:].rearrange("q (b p) -> q b p", p=BLOCK)[:, :, :POSITIONS],
            op0=ALU.min,
            op1=ALU.mult,
        )
        nc.sync.dma_start(
            out=out.rearrange("n (i b) p -> (n i) (b p)", i=BLOCK),
            in_=result[:].rearrange("q b p -> q (b p)"),
        )
